import numpy as np
import ml_dtypes


def mxq(x, axis, fmt="e4m3"):
    dtype, down = {"e4m3": (ml_dtypes.float8_e4m3fn, 7), "e5m2": (ml_dtypes.float8_e5m2, 14)}[fmt]
    v = np.moveaxis(np.asarray(x, np.float32).astype(ml_dtypes.bfloat16).astype(np.float64), axis, -1)
    blocks = v.reshape(v.shape[:-1] + (-1, 32))
    amax = np.abs(blocks).max(-1, keepdims=True)
    byte = np.maximum(np.where(amax > 0, np.frexp(amax)[1] - 1 + 127, 0) - down, 1)
    scale = np.exp2(byte - 127.0)
    codes = (blocks / scale).astype(np.float32).astype(dtype).astype(np.float64)
    return np.moveaxis((codes * scale).reshape(v.shape), -1, axis)


WIDE = False


def mx_kscale(k):
    if not WIDE:
        return np.ones(k)
    levels = np.array([10, -10, 5, -5, 0])
    if k % 512:
        return np.exp2(np.random.permutation(np.resize(levels, k // 32))).repeat(32)
    a = np.empty((k // 512, 16))
    for p in range(k // 512):
        a[p, :8] = np.random.permutation(np.resize(levels, 8))
        for g in range(8):
            far = levels[np.abs(levels - a[p, g]) >= 10]
            a[p, g + 8] = far[np.random.randint(len(far))]
    return np.exp2(a.ravel()).repeat(32)


BF16 = ml_dtypes.bfloat16


def bf(x):
    return np.asarray(x, np.float32).astype(BF16)


def f64(x):
    return np.asarray(x).astype(np.float64)


B, C, H, W, O, K = 2, 512, 8, 16, 256, 3
DIRS = [(0, 1), (1, 1), (1, 0), (1, -1), (0, -1), (-1, -1), (-1, 0), (-1, 1)]
DILATION = 1
CENTER = K // 2
PAD = CENTER * DILATION


def setup_inputs():
    s = mx_kscale(C)
    bound = np.sqrt(6.0 / (C * K))
    return {"x": bf(np.random.standard_normal((B, C, H, W)) * s[None, :, None, None]),
            "weight": bf(np.random.uniform(-bound, bound, (O, C, K)) / s[None, :, None])}


def reference(x, weight):
    xq = mxq(f64(x).reshape(B, C, H * W), 1, "e4m3")
    wq = mxq(f64(weight).transpose(2, 0, 1).reshape(K * O, C), 1, "e4m3")
    y = (wq @ xq).reshape(B, K, O, H, W)
    yp = np.pad(y, ((0, 0), (0, 0), (0, 0), (PAD, PAD), (PAD, PAD)))
    outs = []
    for dy, dx in DIRS:
        acc = np.zeros((B, O, H, W))
        for k in range(K):
            r0 = PAD + (k - CENTER) * DILATION * dy
            c0 = PAD + (k - CENTER) * DILATION * dx
            acc = acc + yp[:, k, :, r0: r0 + H, c0: c0 + W]
        outs.append(acc)
    return np.stack(outs, axis=2)

@@ -1,0 +1,137 @@
+from contextlib import ExitStack
+
+import concourse.mybir as mybir
+from concourse.masks import make_identity
+
+BF16 = mybir.dt.bfloat16
+F32 = mybir.dt.float32
+I32 = mybir.dt.int32
+U32 = mybir.dt.uint32
+U8 = mybir.dt.uint8
+FP8X4 = mybir.dt.float8_e4m3fn_x4
+
+B, C, H, W, O, TAPS = 2, 512, 8, 16, 256, 3
+STEPS = ((0, 1), (1, 1), (1, 0), (1, -1), (0, -1), (-1, -1), (-1, 0), (-1, 1))
+N_STEPS = len(STEPS)
+
+P = 128
+PACK = 4
+PIXELS = H * W
+O_TILES = O // P
+STEPS_PER_BANK = 4
+N_COPIES = N_STEPS + STEPS_PER_BANK
+
+FLOPS = 2 * B * H * W * C * O * TAPS
+
+
+def tile_r8convf_pa_s_kernel(tc, x, weight, out):
+    nc = tc.nc
+    with ExitStack() as ctx:
+        ctx.enter_context(tc.manual_schedule())
+        keep = ctx.enter_context(tc.tile_pool(name="keep", bufs=1))
+        stage = ctx.enter_context(tc.tile_pool(name="stage", bufs=4))
+        psum = ctx.enter_context(tc.psum_pool(name="psum", bufs=8))
+
+        identity = keep.tile([P, P], BF16)
+        x_raw = keep.tile([P, B, PACK, H, W], BF16)
+        w_raw = keep.tile([P, O_TILES, C, TAPS], BF16)
+        x_moved = keep.tile([P, B, 3, H + 2, W, PACK], BF16, align_bytes=64)
+        x_codes = keep.tile([P, B, N_COPIES * PIXELS], U32, align_bytes=64)
+        x_scales = keep.tile([P, B, N_COPIES * PIXELS], U8, align_bytes=64)
+        w_grouped = keep.tile([P, O_TILES, TAPS, P, PACK], BF16, align_bytes=64)
+        w_codes = keep.tile([P, O_TILES, TAPS, P], U32, align_bytes=64)
+        w_scales = keep.tile([P, O_TILES, TAPS, P], U8, align_bytes=64)
+
+        def load_x(b):
+            nc.sync.dma_start(
+                out=x_raw[:, b].rearrange("p t h w -> p t (h w)"),
+                in_=x[b].rearrange("(p t) h w -> p t (h w)", t=PACK),
+            )
+
+        def load_weight(ot):
+            nc.sync.dma_start(
+                out=w_raw[:, ot].rearrange("p c k -> p (c k)"),
+                in_=weight[ot * P : (ot + 1) * P].rearrange("o c k -> o (c k)"),
+            )
+
+        def move_x(b):
+            for dx in (-1, 0, 1):
+                first, last = max(0, -dx), W - max(0, dx)
+                nc.vector.tensor_copy(
+                    out=x_moved[:, b, dx + 1, 1 : 1 + H, first:last, :],
+                    in_=x_raw[:, b, :, :, first + dx : last + dx].rearrange("p t h w -> p h w t"),
+                )
+
+        def quantise_copy(b, copy, dy, dx):
+            columns = slice(copy * PIXELS, (copy + 1) * PIXELS)
+            nc.vector.quantize_mx(
+                out=x_codes[:, b, columns].bitcast(FP8X4),
+                scales=x_scales[:, b, columns],
+                in_=x_moved[:, b, dx + 1, 1 + dy : 1 + dy + H].rearrange("p h w t -> p (h w t)"),
+            )
+
+        def quantise_x(b):
+            for d, (dy, dx) in enumerate(STEPS):
+                quantise_copy(b, d, dy, dx)
+            for copy in range(N_STEPS, N_COPIES):
+                quantise_copy(b, copy, 0, 0)
+
+        def transpose_weight(ot):
+            for k in range(TAPS):
+                w_t = psum.tile([P, PACK, P], BF16, tag="bank", name="w_t")
+                for t in range(PACK):
+                    nc.tensor.transpose(w_t[:, t, :], w_raw[:, ot, t : C : PACK, k], identity[:])
+                nc.scalar.copy(out=w_grouped[:, ot, k], in_=w_t[:].rearrange("p t o -> p o t"))
+
+        def quantise_weight(ot):
+            for k in range(TAPS):
+                nc.vector.quantize_mx(
+                    out=w_codes[:, ot, k].bitcast(FP8X4),
+                    scales=w_scales[:, ot, k],
+                    in_=w_grouped[:, ot, k].rearrange("p o t -> p (o t)"),
+                )
+
+        def convolve(ot, b):
+            for d0 in range(0, N_STEPS, STEPS_PER_BANK):
+                first_copy = {0: (d0 + N_STEPS // 2) % N_STEPS, 1: N_STEPS, 2: d0}
+                acc = psum.tile([P, STEPS_PER_BANK * PIXELS], F32, tag="bank", name="acc")
+                for k in range(TAPS):
+                    columns = slice(first_copy[k] * PIXELS, (first_copy[k] + STEPS_PER_BANK) * PIXELS)
+                    nc.tensor.matmul_mx(
+                        out=acc[:],
+                        lhsT=w_codes[:, ot, k].bitcast(FP8X4),
+                        lhsT_scale=w_scales[:, ot, k],
+                        rhs=x_codes[:, b, columns].bitcast(FP8X4),
+                        rhs_scale=x_scales[:, b, columns],
+                        start=(k == 0),
+                        stop=(k == TAPS - 1),
+                    )
+                result = stage.tile([P, STEPS_PER_BANK * PIXELS], F32)
+                nc.scalar.copy(out=result[:], in_=acc[:])
+                nc.sync.dma_start(
+                    out=out[b, ot * P : (ot + 1) * P, d0 : d0 + STEPS_PER_BANK].rearrange(
+                        "o d h w -> o (d h w)"
+                    ),
+                    in_=result[:],
+                )
+
+        load_x(0)
+        load_weight(0)
+        load_weight(1)
+        load_x(1)
+        make_identity(nc, identity[:])
+        for b in range(B):
+            nc.vector.memset(x_moved[:, b].rearrange("p a h w t -> p (a h w t)").bitcast(I32), 0)
+
+        move_x(0)
+        transpose_weight(0)
+        quantise_x(0)
+        transpose_weight(1)
+        quantise_weight(0)
+        move_x(1)
+        quantise_weight(1)
+        convolve(0, 0)
+        convolve(1, 0)
+        quantise_x(1)
+        convolve(0, 1)
+        convolve(1, 1)

@@ -32,12 +32,13 @@ def tile_r8convf_pa_s_kernel(tc, x, weight, out):
         stage = ctx.enter_context(tc.tile_pool(name="stage", bufs=4))
         psum = ctx.enter_context(tc.psum_pool(name="psum", bufs=8))
 
-        identity = keep.tile([P, P], BF16)
+        identity = keep.tile([P, P], F32)
         x_raw = keep.tile([P, B, PACK, H, W], BF16)
         w_raw = keep.tile([P, O_TILES, C, TAPS], BF16)
         x_moved = keep.tile([P, B, 3, H + 2, W, PACK], BF16, align_bytes=64)
         x_codes = keep.tile([P, B, N_COPIES * PIXELS], U32, align_bytes=64)
         x_scales = keep.tile([P, B, N_COPIES * PIXELS], U8, align_bytes=64)
+        w_pairs = keep.tile([P, O_TILES, TAPS, PACK // 2, P, 2], BF16, align_bytes=64)
         w_grouped = keep.tile([P, O_TILES, TAPS, P, PACK], BF16, align_bytes=64)
         w_codes = keep.tile([P, O_TILES, TAPS, P], U32, align_bytes=64)
         w_scales = keep.tile([P, O_TILES, TAPS, P], U8, align_bytes=64)
@@ -70,18 +71,33 @@ def tile_r8convf_pa_s_kernel(tc, x, weight, out):
                 in_=x_moved[:, b, dx + 1, 1 + dy : 1 + dy + H].rearrange("p h w t -> p (h w t)"),
             )
 
-        def quantise_x(b):
-            for d, (dy, dx) in enumerate(STEPS):
-                quantise_copy(b, d, dy, dx)
+        def quantise_moved(b, d0):
+            for d in range(d0, d0 + STEPS_PER_BANK):
+                quantise_copy(b, d, *STEPS[d])
+
+        def quantise_unmoved(b):
             for copy in range(N_STEPS, N_COPIES):
                 quantise_copy(b, copy, 0, 0)
 
+        def sort_weight(ot):
+            for k in range(TAPS):
+                pairs = w_raw[:, ot, :, k].rearrange("o (p u e) -> o u p e", u=PACK // 2, e=2)
+                if k == 1:
+                    nc.scalar.copy(out=w_pairs[:, ot, k], in_=pairs)
+                else:
+                    nc.vector.tensor_copy(out=w_pairs[:, ot, k], in_=pairs)
+
         def transpose_weight(ot):
             for k in range(TAPS):
-                w_t = psum.tile([P, PACK, P], BF16, tag="bank", name="w_t")
-                for t in range(PACK):
-                    nc.tensor.transpose(w_t[:, t, :], w_raw[:, ot, t : C : PACK, k], identity[:])
-                nc.scalar.copy(out=w_grouped[:, ot, k], in_=w_t[:].rearrange("p t o -> p o t"))
+                w_t = psum.tile([P, PACK // 2, P], F32, tag="bank", name="w_t")
+                for u in range(PACK // 2):
+                    words = w_pairs[:, ot, k, u].rearrange("o p e -> o (p e)").bitcast(F32)
+                    nc.tensor.transpose(w_t[:, u, :], words, identity[:])
+                grouped_words = w_grouped[:, ot, k].rearrange("p o t -> p (o t)").bitcast(F32)
+                nc.scalar.copy(
+                    out=grouped_words.rearrange("p (o u) -> p o u", u=PACK // 2),
+                    in_=w_t[:].rearrange("p u o -> p o u"),
+                )
 
         def quantise_weight(ot):
             for k in range(TAPS):
@@ -92,20 +108,30 @@ def tile_r8convf_pa_s_kernel(tc, x, weight, out):
                 )
 
         def convolve(ot, b):
-            for d0 in range(0, N_STEPS, STEPS_PER_BANK):
-                first_copy = {0: (d0 + N_STEPS // 2) % N_STEPS, 1: N_STEPS, 2: d0}
-                acc = psum.tile([P, STEPS_PER_BANK * PIXELS], F32, tag="bank", name="acc")
-                for k in range(TAPS):
-                    columns = slice(first_copy[k] * PIXELS, (first_copy[k] + STEPS_PER_BANK) * PIXELS)
+            halves = range(0, N_STEPS, STEPS_PER_BANK)
+            accs = {}
+            for d0 in halves:
+                accs[d0] = psum.tile([P, STEPS_PER_BANK * PIXELS], F32, tag="bank", name="acc")
+            for first_copy in (0, STEPS_PER_BANK, N_STEPS):
+                for d0 in halves:
+                    if first_copy == N_STEPS:
+                        k = 1
+                    elif first_copy == d0:
+                        k = 2
+                    else:
+                        k = 0
+                    columns = slice(first_copy * PIXELS, (first_copy + STEPS_PER_BANK) * PIXELS)
                     nc.tensor.matmul_mx(
-                        out=acc[:],
+                        out=accs[d0][:],
                         lhsT=w_codes[:, ot, k].bitcast(FP8X4),
                         lhsT_scale=w_scales[:, ot, k],
                         rhs=x_codes[:, b, columns].bitcast(FP8X4),
                         rhs_scale=x_scales[:, b, columns],
-                        start=(k == 0),
-                        stop=(k == TAPS - 1),
+                        start=(first_copy == 0),
+                        stop=(first_copy == N_STEPS),
                     )
+            for d0 in halves:
+                acc = accs[d0]
                 result = stage.tile([P, STEPS_PER_BANK * PIXELS], F32)
                 nc.scalar.copy(out=result[:], in_=acc[:])
                 nc.sync.dma_start(
@@ -124,14 +150,20 @@ def tile_r8convf_pa_s_kernel(tc, x, weight, out):
             nc.vector.memset(x_moved[:, b].rearrange("p a h w t -> p (a h w t)").bitcast(I32), 0)
 
         move_x(0)
+        sort_weight(0)
         transpose_weight(0)
-        quantise_x(0)
+        quantise_moved(0, 0)
+        sort_weight(1)
         transpose_weight(1)
         quantise_weight(0)
-        move_x(1)
+        quantise_moved(0, STEPS_PER_BANK)
+        quantise_unmoved(0)
         quantise_weight(1)
         convolve(0, 0)
+        move_x(1)
         convolve(1, 0)
-        quantise_x(1)
+        quantise_moved(1, 0)
+        quantise_moved(1, STEPS_PER_BANK)
+        quantise_unmoved(1)
         convolve(0, 1)
         convolve(1, 1)

@@ -20,6 +20,7 @@ PIXELS = H * W
 O_TILES = O // P
 STEPS_PER_BANK = 4
 N_COPIES = N_STEPS + STEPS_PER_BANK
+HALVES = (0, STEPS_PER_BANK)
 
 FLOPS = 2 * B * H * W * C * O * TAPS
 
@@ -29,10 +30,12 @@ def tile_r8convf_pa_s_kernel(tc, x, weight, out):
     with ExitStack() as ctx:
         ctx.enter_context(tc.manual_schedule())
         keep = ctx.enter_context(tc.tile_pool(name="keep", bufs=1))
-        stage = ctx.enter_context(tc.tile_pool(name="stage", bufs=4))
+        stage = ctx.enter_context(tc.tile_pool(name="stage", bufs=8))
+        mid_pool = ctx.enter_context(tc.tile_pool(name="mid_pool", bufs=4))
         psum = ctx.enter_context(tc.psum_pool(name="psum", bufs=8))
 
         identity = keep.tile([P, P], F32)
+        identity_bf16 = keep.tile([P, P], BF16)
         x_raw = keep.tile([P, B, PACK, H, W], BF16)
         w_raw = keep.tile([P, O_TILES, C, TAPS], BF16)
         x_moved = keep.tile([P, B, 3, H + 2, W, PACK], BF16, align_bytes=64)
@@ -55,12 +58,15 @@ def tile_r8convf_pa_s_kernel(tc, x, weight, out):
                 in_=weight[ot * P : (ot + 1) * P].rearrange("o c k -> o (c k)"),
             )
 
-        def move_x(b):
-            for dx in (-1, 0, 1):
+        def interleave_x(b, copy_on_engine):
+            copy_on_engine(out=x_moved[:, b, 1, 1 : 1 + H], in_=x_raw[:, b].rearrange("p t h w -> p h w t"))
+
+        def shift_x(b):
+            for dx in (1, -1):
                 first, last = max(0, -dx), W - max(0, dx)
-                nc.vector.tensor_copy(
-                    out=x_moved[:, b, dx + 1, 1 : 1 + H, first:last, :],
-                    in_=x_raw[:, b, :, :, first + dx : last + dx].rearrange("p t h w -> p h w t"),
+                nc.scalar.copy(
+                    out=x_moved[:, b, dx + 1, 1 : 1 + H, first:last],
+                    in_=x_moved[:, b, 1, 1 : 1 + H, first + dx : last + dx],
                 )
 
         def quantise_copy(b, copy, dy, dx):
@@ -71,99 +77,150 @@ def tile_r8convf_pa_s_kernel(tc, x, weight, out):
                 in_=x_moved[:, b, dx + 1, 1 + dy : 1 + dy + H].rearrange("p h w t -> p (h w t)"),
             )
 
-        def quantise_moved(b, d0):
-            for d in range(d0, d0 + STEPS_PER_BANK):
+        def quantise_steps(b, steps):
+            for d in steps:
                 quantise_copy(b, d, *STEPS[d])
 
-        def quantise_unmoved(b):
-            for copy in range(N_STEPS, N_COPIES):
+        def quantise_unmoved(b, n):
+            for copy in range(N_STEPS, N_STEPS + n):
                 quantise_copy(b, copy, 0, 0)
 
-        def sort_weight(ot):
-            for k in range(TAPS):
-                pairs = w_raw[:, ot, :, k].rearrange("o (p u e) -> o u p e", u=PACK // 2, e=2)
-                if k == 1:
-                    nc.scalar.copy(out=w_pairs[:, ot, k], in_=pairs)
-                else:
-                    nc.vector.tensor_copy(out=w_pairs[:, ot, k], in_=pairs)
+        def sort_weight(ot, k, copy_on_engine):
+            copy_on_engine(
+                out=w_pairs[:, ot, k],
+                in_=w_raw[:, ot, :, k].rearrange("o (p u e) -> o u p e", u=PACK // 2, e=2),
+            )
 
-        def transpose_weight(ot):
-            for k in range(TAPS):
-                w_t = psum.tile([P, PACK // 2, P], F32, tag="bank", name="w_t")
-                for u in range(PACK // 2):
-                    words = w_pairs[:, ot, k, u].rearrange("o p e -> o (p e)").bitcast(F32)
-                    nc.tensor.transpose(w_t[:, u, :], words, identity[:])
-                grouped_words = w_grouped[:, ot, k].rearrange("p o t -> p (o t)").bitcast(F32)
-                nc.scalar.copy(
-                    out=grouped_words.rearrange("p (o u) -> p o u", u=PACK // 2),
-                    in_=w_t[:].rearrange("p u o -> p o u"),
-                )
+        def transpose_unsorted_weight(ot, k):
+            w_t = psum.tile([P, PACK, P], BF16, tag="bank", name="w_t")
+            for t in range(PACK):
+                nc.tensor.transpose(w_t[:, t, :], w_raw[:, ot, t : C : PACK, k], identity_bf16[:])
+            nc.scalar.copy(out=w_grouped[:, ot, k], in_=w_t[:].rearrange("p t o -> p o t"))
 
-        def quantise_weight(ot):
-            for k in range(TAPS):
-                nc.vector.quantize_mx(
-                    out=w_codes[:, ot, k].bitcast(FP8X4),
-                    scales=w_scales[:, ot, k],
-                    in_=w_grouped[:, ot, k].rearrange("p o t -> p (o t)"),
-                )
+        def transpose_sorted_weight(ot, k):
+            w_t = psum.tile([P, PACK // 2, P], F32, tag="bank", name="w_t")
+            for u in range(PACK // 2):
+                words = w_pairs[:, ot, k, u].rearrange("o p e -> o (p e)").bitcast(F32)
+                nc.tensor.transpose(w_t[:, u, :], words, identity[:])
+            grouped_words = w_grouped[:, ot, k].rearrange("p o t -> p (o t)").bitcast(F32)
+            nc.scalar.copy(
+                out=grouped_words.rearrange("p (o u) -> p o u", u=PACK // 2),
+                in_=w_t[:].rearrange("p u o -> p o u"),
+            )
 
-        def convolve(ot, b):
-            halves = range(0, N_STEPS, STEPS_PER_BANK)
-            accs = {}
-            for d0 in halves:
-                accs[d0] = psum.tile([P, STEPS_PER_BANK * PIXELS], F32, tag="bank", name="acc")
-            for first_copy in (0, STEPS_PER_BANK, N_STEPS):
-                for d0 in halves:
-                    if first_copy == N_STEPS:
-                        k = 1
-                    elif first_copy == d0:
-                        k = 2
-                    else:
-                        k = 0
-                    columns = slice(first_copy * PIXELS, (first_copy + STEPS_PER_BANK) * PIXELS)
-                    nc.tensor.matmul_mx(
-                        out=accs[d0][:],
-                        lhsT=w_codes[:, ot, k].bitcast(FP8X4),
-                        lhsT_scale=w_scales[:, ot, k],
-                        rhs=x_codes[:, b, columns].bitcast(FP8X4),
-                        rhs_scale=x_scales[:, b, columns],
-                        start=(first_copy == 0),
-                        stop=(first_copy == N_STEPS),
-                    )
-            for d0 in halves:
-                acc = accs[d0]
-                result = stage.tile([P, STEPS_PER_BANK * PIXELS], F32)
-                nc.scalar.copy(out=result[:], in_=acc[:])
-                nc.sync.dma_start(
-                    out=out[b, ot * P : (ot + 1) * P, d0 : d0 + STEPS_PER_BANK].rearrange(
-                        "o d h w -> o (d h w)"
-                    ),
-                    in_=result[:],
-                )
+        def quantise_weight(ot, k):
+            nc.vector.quantize_mx(
+                out=w_codes[:, ot, k].bitcast(FP8X4),
+                scales=w_scales[:, ot, k],
+                in_=w_grouped[:, ot, k].rearrange("p o t -> p (o t)"),
+            )
+
+        def new_bank():
+            acc = psum.tile([P, STEPS_PER_BANK, PIXELS], F32, tag="bank", name="acc")
+            return acc
+
+        def multiply(acc, ot, b, k, first_copy, copies, start, stop):
+            columns = slice(first_copy * PIXELS, (first_copy + copies) * PIXELS)
+            nc.tensor.matmul_mx(
+                out=acc[:, :copies].rearrange("p d n -> p (d n)"),
+                lhsT=w_codes[:, ot, k].bitcast(FP8X4),
+                lhsT_scale=w_scales[:, ot, k],
+                rhs=x_codes[:, b, columns].bitcast(FP8X4),
+                rhs_scale=x_scales[:, b, columns],
+                start=start,
+                stop=stop,
+            )
+
+        def store(ot, b, d0, result):
+            nc.sync.dma_start(
+                out=out[b, ot * P : (ot + 1) * P, d0 : d0 + STEPS_PER_BANK].rearrange("o d h w -> o d (h w)"),
+                in_=result[:],
+            )
+
+        def finish_on_scalar(ot, b, d0, acc):
+            result = stage.tile([P, STEPS_PER_BANK, PIXELS], F32, tag="result", name="result")
+            nc.scalar.copy(out=result[:], in_=acc[:])
+            store(ot, b, d0, result)
+
+        def outer_taps(ot, b, accs, first_copy, start, stop):
+            multiply(accs[first_copy], ot, b, 2, first_copy, STEPS_PER_BANK, start, stop)
+            multiply(accs[(first_copy + STEPS_PER_BANK) % N_STEPS], ot, b, 0, first_copy, STEPS_PER_BANK, start, stop)
+
+        def multiply_middle(ot, b):
+            product = psum.tile([P, STEPS_PER_BANK, PIXELS], F32, tag="bank", name="product")
+            multiply(product, ot, b, 1, N_STEPS, 1, True, True)
+            middle = mid_pool.tile([P, 1, PIXELS], F32, tag="middle", name="middle")
+            nc.scalar.copy(out=middle[:], in_=product[:, :1])
+            return middle
+
+        def finish_on_vector(ot, b, d0, acc, middle):
+            result = stage.tile([P, STEPS_PER_BANK, PIXELS], F32, tag="result", name="result")
+            nc.vector.tensor_tensor(
+                out=result[:],
+                in0=acc[:],
+                in1=middle[:].to_broadcast([P, STEPS_PER_BANK, PIXELS]),
+                op=mybir.AluOpType.add,
+            )
+            store(ot, b, d0, result)
+
+        def outer_taps_of_bank(ot, b, d0):
+            acc = new_bank()
+            multiply(acc, ot, b, 2, d0, STEPS_PER_BANK, True, False)
+            multiply(acc, ot, b, 0, (d0 + STEPS_PER_BANK) % N_STEPS, STEPS_PER_BANK, False, True)
+            return acc
 
         load_x(0)
         load_weight(0)
         load_weight(1)
         load_x(1)
+        make_identity(nc, identity_bf16[:])
         make_identity(nc, identity[:])
         for b in range(B):
             nc.vector.memset(x_moved[:, b].rearrange("p a h w t -> p (a h w t)").bitcast(I32), 0)
 
-        move_x(0)
-        sort_weight(0)
-        transpose_weight(0)
-        quantise_moved(0, 0)
-        sort_weight(1)
-        transpose_weight(1)
-        quantise_weight(0)
-        quantise_moved(0, STEPS_PER_BANK)
-        quantise_unmoved(0)
-        quantise_weight(1)
-        convolve(0, 0)
-        move_x(1)
-        convolve(1, 0)
-        quantise_moved(1, 0)
-        quantise_moved(1, STEPS_PER_BANK)
-        quantise_unmoved(1)
-        convolve(0, 1)
-        convolve(1, 1)
+        vector_copy, scalar_copy = nc.vector.tensor_copy, nc.scalar.copy
+        interleave_x(0, vector_copy)
+        shift_x(0)
+        transpose_unsorted_weight(0, 1)
+        sort_weight(0, 0, vector_copy)
+        sort_weight(0, 2, vector_copy)
+        for k in (0, 2):
+            transpose_sorted_weight(0, k)
+        quantise_steps(0, (2, 6))
+        transpose_unsorted_weight(1, 1)
+        sort_weight(1, 0, vector_copy)
+        sort_weight(1, 2, vector_copy)
+        for k in (0, 2):
+            transpose_sorted_weight(1, k)
+        quantise_steps(0, (0, 1, 3))
+        quantise_weight(0, 0)
+        quantise_weight(0, 2)
+        quantise_steps(0, (4, 5, 7))
+        quantise_weight(0, 1)
+        quantise_unmoved(0, STEPS_PER_BANK)
+        for k in (0, 2, 1):
+            quantise_weight(1, k)
+        interleave_x(1, scalar_copy)
+        shift_x(1)
+        quantise_unmoved(1, 1)
+        quantise_steps(1, (2, 6, 0, 1, 3, 4, 5, 7))
+
+        banks = {d0: new_bank() for d0 in HALVES}
+        outer_taps(0, 0, banks, 0, True, False)
+        outer_taps(0, 0, banks, STEPS_PER_BANK, False, False)
+        for d0 in HALVES:
+            multiply(banks[d0], 0, 0, 1, N_STEPS, STEPS_PER_BANK, False, True)
+            finish_on_scalar(0, 0, d0, banks[d0])
+        middle = multiply_middle(1, 0)
+        acc = new_bank()
+        multiply(acc, 1, 0, 2, 0, STEPS_PER_BANK, True, False)
+        multiply(acc, 1, 0, 0, STEPS_PER_BANK, STEPS_PER_BANK, False, False)
+        multiply(acc, 1, 0, 1, N_STEPS, STEPS_PER_BANK, False, True)
+        finish_on_scalar(1, 0, 0, acc)
+        acc = outer_taps_of_bank(1, 0, STEPS_PER_BANK)
+        finish_on_vector(1, 0, STEPS_PER_BANK, acc, middle)
+        middles = [multiply_middle(ot, 1) for ot in range(O_TILES)]
+        for ot in range(O_TILES):
+            for d0 in HALVES:
+                acc = outer_taps_of_bank(ot, 1, d0)
+                finish_on_vector(ot, 1, d0, acc, middles[ot])

@@ -34,6 +34,7 @@ def tile_r8convf_pa_s_kernel(tc, x, weight, out):
         mid_pool = ctx.enter_context(tc.tile_pool(name="mid_pool", bufs=4))
         psum = ctx.enter_context(tc.psum_pool(name="psum", bufs=8))
 
+        zeros = keep.tile([P, STEPS_PER_BANK * PIXELS], F32)
         identity = keep.tile([P, P], F32)
         identity_bf16 = keep.tile([P, P], BF16)
         x_raw = keep.tile([P, B, PACK, H, W], BF16)
@@ -173,6 +174,9 @@ def tile_r8convf_pa_s_kernel(tc, x, weight, out):
         load_weight(0)
         load_weight(1)
         load_x(1)
+        nc.vector.memset(zeros[:], 0.0)
+        unused = psum.tile([P, STEPS_PER_BANK * PIXELS], F32, tag="bank", name="unused")
+        nc.tensor.matmul(unused[:], zeros[:, :P], zeros[:], start=True, stop=True)
         make_identity(nc, identity_bf16[:])
         make_identity(nc, identity[:])
         for b in range(B):

@@ -19,7 +19,8 @@ PACK = 4
 PIXELS = H * W
 O_TILES = O // P
 STEPS_PER_BANK = 4
-N_COPIES = N_STEPS + STEPS_PER_BANK
+UNMOVED = N_STEPS
+N_COPIES = N_STEPS + 1
 HALVES = (0, STEPS_PER_BANK)
 
 FLOPS = 2 * B * H * W * C * O * TAPS
@@ -34,7 +35,7 @@ def tile_r8convf_pa_s_kernel(tc, x, weight, out):
         mid_pool = ctx.enter_context(tc.tile_pool(name="mid_pool", bufs=4))
         psum = ctx.enter_context(tc.psum_pool(name="psum", bufs=8))
 
-        zeros = keep.tile([P, STEPS_PER_BANK * PIXELS], F32)
+        zeros = keep.tile([P, P], F32)
         identity = keep.tile([P, P], F32)
         identity_bf16 = keep.tile([P, P], BF16)
         x_raw = keep.tile([P, B, PACK, H, W], BF16)
@@ -62,13 +63,12 @@ def tile_r8convf_pa_s_kernel(tc, x, weight, out):
         def interleave_x(b, copy_on_engine):
             copy_on_engine(out=x_moved[:, b, 1, 1 : 1 + H], in_=x_raw[:, b].rearrange("p t h w -> p h w t"))
 
-        def shift_x(b):
-            for dx in (1, -1):
-                first, last = max(0, -dx), W - max(0, dx)
-                nc.scalar.copy(
-                    out=x_moved[:, b, dx + 1, 1 : 1 + H, first:last],
-                    in_=x_moved[:, b, 1, 1 : 1 + H, first + dx : last + dx],
-                )
+        def shift_x(b, dx, copy_on_engine):
+            first, last = max(0, -dx), W - max(0, dx)
+            copy_on_engine(
+                out=x_moved[:, b, dx + 1, 1 : 1 + H, first:last],
+                in_=x_moved[:, b, 1, 1 : 1 + H, first + dx : last + dx],
+            )
 
         def quantise_copy(b, copy, dy, dx):
             columns = slice(copy * PIXELS, (copy + 1) * PIXELS)
@@ -82,9 +82,8 @@ def tile_r8convf_pa_s_kernel(tc, x, weight, out):
             for d in steps:
                 quantise_copy(b, d, *STEPS[d])
 
-        def quantise_unmoved(b, n):
-            for copy in range(N_STEPS, N_STEPS + n):
-                quantise_copy(b, copy, 0, 0)
+        def quantise_unmoved(b):
+            quantise_copy(b, UNMOVED, 0, 0)
 
         def sort_weight(ot, k, copy_on_engine):
             copy_on_engine(
@@ -96,6 +95,9 @@ def tile_r8convf_pa_s_kernel(tc, x, weight, out):
             w_t = psum.tile([P, PACK, P], BF16, tag="bank", name="w_t")
             for t in range(PACK):
                 nc.tensor.transpose(w_t[:, t, :], w_raw[:, ot, t : C : PACK, k], identity_bf16[:])
+            return w_t
+
+        def group_unsorted_weight(ot, k, w_t):
             nc.scalar.copy(out=w_grouped[:, ot, k], in_=w_t[:].rearrange("p t o -> p o t"))
 
         def transpose_sorted_weight(ot, k):
@@ -103,6 +105,9 @@ def tile_r8convf_pa_s_kernel(tc, x, weight, out):
             for u in range(PACK // 2):
                 words = w_pairs[:, ot, k, u].rearrange("o p e -> o (p e)").bitcast(F32)
                 nc.tensor.transpose(w_t[:, u, :], words, identity[:])
+            return w_t
+
+        def group_sorted_weight(ot, k, w_t):
             grouped_words = w_grouped[:, ot, k].rearrange("p o t -> p (o t)").bitcast(F32)
             nc.scalar.copy(
                 out=grouped_words.rearrange("p (o u) -> p o u", u=PACK // 2),
@@ -120,10 +125,10 @@ def tile_r8convf_pa_s_kernel(tc, x, weight, out):
             acc = psum.tile([P, STEPS_PER_BANK, PIXELS], F32, tag="bank", name="acc")
             return acc
 
-        def multiply(acc, ot, b, k, first_copy, copies, start, stop):
-            columns = slice(first_copy * PIXELS, (first_copy + copies) * PIXELS)
+        def multiply(product, ot, b, k, first_copy, start, stop):
+            columns = slice(first_copy * PIXELS, (first_copy + product.shape[1]) * PIXELS)
             nc.tensor.matmul_mx(
-                out=acc[:, :copies].rearrange("p d n -> p (d n)"),
+                out=product.rearrange("p d n -> p (d n)"),
                 lhsT=w_codes[:, ot, k].bitcast(FP8X4),
                 lhsT_scale=w_scales[:, ot, k],
                 rhs=x_codes[:, b, columns].bitcast(FP8X4),
@@ -133,8 +138,9 @@ def tile_r8convf_pa_s_kernel(tc, x, weight, out):
             )
 
         def store(ot, b, d0, result):
+            n = result.shape[1]
             nc.sync.dma_start(
-                out=out[b, ot * P : (ot + 1) * P, d0 : d0 + STEPS_PER_BANK].rearrange("o d h w -> o d (h w)"),
+                out=out[b, ot * P : (ot + 1) * P, d0 : d0 + n].rearrange("o d h w -> o d (h w)"),
                 in_=result[:],
             )
 
@@ -143,31 +149,31 @@ def tile_r8convf_pa_s_kernel(tc, x, weight, out):
             nc.scalar.copy(out=result[:], in_=acc[:])
             store(ot, b, d0, result)
 
-        def outer_taps(ot, b, accs, first_copy, start, stop):
-            multiply(accs[first_copy], ot, b, 2, first_copy, STEPS_PER_BANK, start, stop)
-            multiply(accs[(first_copy + STEPS_PER_BANK) % N_STEPS], ot, b, 0, first_copy, STEPS_PER_BANK, start, stop)
+        def add_middle_in_psum(ot, b, acc):
+            for i in range(STEPS_PER_BANK):
+                multiply(acc[:, i : i + 1], ot, b, 1, UNMOVED, False, i == STEPS_PER_BANK - 1)
 
         def multiply_middle(ot, b):
-            product = psum.tile([P, STEPS_PER_BANK, PIXELS], F32, tag="bank", name="product")
-            multiply(product, ot, b, 1, N_STEPS, 1, True, True)
+            product = new_bank()
+            multiply(product[:, :1], ot, b, 1, UNMOVED, True, True)
             middle = mid_pool.tile([P, 1, PIXELS], F32, tag="middle", name="middle")
             nc.scalar.copy(out=middle[:], in_=product[:, :1])
             return middle
 
-        def finish_on_vector(ot, b, d0, acc, middle):
-            result = stage.tile([P, STEPS_PER_BANK, PIXELS], F32, tag="result", name="result")
+        def finish_on_vector(ot, b, d0, acc, middle, n=STEPS_PER_BANK):
+            result = stage.tile([P, n, PIXELS], F32, tag="result", name="result")
             nc.vector.tensor_tensor(
                 out=result[:],
-                in0=acc[:],
-                in1=middle[:].to_broadcast([P, STEPS_PER_BANK, PIXELS]),
+                in0=acc[:, :n],
+                in1=middle[:].to_broadcast([P, n, PIXELS]),
                 op=mybir.AluOpType.add,
             )
             store(ot, b, d0, result)
 
-        def outer_taps_of_bank(ot, b, d0):
+        def outer_taps(ot, b, d0, stop, n=STEPS_PER_BANK):
             acc = new_bank()
-            multiply(acc, ot, b, 2, d0, STEPS_PER_BANK, True, False)
-            multiply(acc, ot, b, 0, (d0 + STEPS_PER_BANK) % N_STEPS, STEPS_PER_BANK, False, True)
+            multiply(acc[:, :n], ot, b, 2, d0, True, False)
+            multiply(acc[:, :n], ot, b, 0, (d0 + N_STEPS // 2) % N_STEPS, False, stop)
             return acc
 
         load_x(0)
@@ -175,56 +181,66 @@ def tile_r8convf_pa_s_kernel(tc, x, weight, out):
         load_weight(1)
         load_x(1)
         nc.vector.memset(zeros[:], 0.0)
-        unused = psum.tile([P, STEPS_PER_BANK * PIXELS], F32, tag="bank", name="unused")
-        nc.tensor.matmul(unused[:], zeros[:, :P], zeros[:], start=True, stop=True)
+        unused = psum.tile([P, STEPS_PER_BANK, P], F32, tag="bank", name="unused")
+        for i in range(STEPS_PER_BANK):
+            nc.tensor.matmul(unused[:, i], zeros[:], zeros[:], start=True, stop=True)
         make_identity(nc, identity_bf16[:])
         make_identity(nc, identity[:])
-        for b in range(B):
-            nc.vector.memset(x_moved[:, b].rearrange("p a h w t -> p (a h w t)").bitcast(I32), 0)
+        borders = x_moved[:].rearrange("p b a h w t -> p (b a) h (w t)").bitcast(I32)
+        nc.vector.memset(borders[:, :, 0 : H + 2 : H + 1], 0)
+        nc.vector.memset(borders[:, 0 : 3 * B : 3, 1 : 1 + H, :2], 0)
+        nc.vector.memset(borders[:, 2 : 3 * B : 3, 1 : 1 + H, 2 * W - 2 :], 0)
 
         vector_copy, scalar_copy = nc.vector.tensor_copy, nc.scalar.copy
         interleave_x(0, vector_copy)
-        shift_x(0)
-        transpose_unsorted_weight(0, 1)
-        sort_weight(0, 0, vector_copy)
-        sort_weight(0, 2, vector_copy)
-        for k in (0, 2):
-            transpose_sorted_weight(0, k)
-        quantise_steps(0, (2, 6))
-        transpose_unsorted_weight(1, 1)
-        sort_weight(1, 0, vector_copy)
+        shift_x(0, -1, scalar_copy)
+        shift_x(0, 1, vector_copy)
+        unsorted = transpose_unsorted_weight(0, 1)
+        for k in (2, 0):
+            sort_weight(0, k, vector_copy)
+        for k in (2, 0):
+            group_sorted_weight(0, k, transpose_sorted_weight(0, k))
+        group_unsorted_weight(0, 1, unsorted)
+        quantise_steps(0, (2, 0, 1, 3))
+        for k in (0, 1):
+            group_unsorted_weight(1, k, transpose_unsorted_weight(1, k))
         sort_weight(1, 2, vector_copy)
-        for k in (0, 2):
-            transpose_sorted_weight(1, k)
-        quantise_steps(0, (0, 1, 3))
-        quantise_weight(0, 0)
+        group_sorted_weight(1, 2, transpose_sorted_weight(1, 2))
         quantise_weight(0, 2)
-        quantise_steps(0, (4, 5, 7))
+        quantise_weight(0, 0)
+        quantise_steps(0, (6, 7, 4, 5))
         quantise_weight(0, 1)
-        quantise_unmoved(0, STEPS_PER_BANK)
-        for k in (0, 2, 1):
-            quantise_weight(1, k)
-        interleave_x(1, scalar_copy)
-        shift_x(1)
-        quantise_unmoved(1, 1)
-        quantise_steps(1, (2, 6, 0, 1, 3, 4, 5, 7))
+        quantise_unmoved(0)
+        interleave_x(1, vector_copy)
+        shift_x(1, 1, scalar_copy)
 
-        banks = {d0: new_bank() for d0 in HALVES}
-        outer_taps(0, 0, banks, 0, True, False)
-        outer_taps(0, 0, banks, STEPS_PER_BANK, False, False)
-        for d0 in HALVES:
-            multiply(banks[d0], 0, 0, 1, N_STEPS, STEPS_PER_BANK, False, True)
-            finish_on_scalar(0, 0, d0, banks[d0])
+        first, second = new_bank(), new_bank()
+        multiply(first[:], 0, 0, 2, 0, True, False)
+        multiply(second[:], 0, 0, 0, 0, True, False)
+        multiply(first[:], 0, 0, 0, STEPS_PER_BANK, False, False)
+        multiply(second[:], 0, 0, 2, STEPS_PER_BANK, False, False)
+        for d0, acc in zip(HALVES, (first, second)):
+            add_middle_in_psum(0, 0, acc)
+            finish_on_scalar(0, 0, d0, acc)
+            if d0 == 0:
+                shift_x(1, -1, scalar_copy)
+
+        for k in (2, 0, 1):
+            quantise_weight(1, k)
+        quantise_unmoved(1)
+        quantise_steps(1, (2, 6, 0, 1, 7, 3, 4, 5))
+
+        first = outer_taps(1, 0, 0, False)
         middle = multiply_middle(1, 0)
-        acc = new_bank()
-        multiply(acc, 1, 0, 2, 0, STEPS_PER_BANK, True, False)
-        multiply(acc, 1, 0, 0, STEPS_PER_BANK, STEPS_PER_BANK, False, False)
-        multiply(acc, 1, 0, 1, N_STEPS, STEPS_PER_BANK, False, True)
-        finish_on_scalar(1, 0, 0, acc)
-        acc = outer_taps_of_bank(1, 0, STEPS_PER_BANK)
-        finish_on_vector(1, 0, STEPS_PER_BANK, acc, middle)
+        add_middle_in_psum(1, 0, first)
+        finish_on_scalar(1, 0, 0, first)
+        finish_on_vector(1, 0, STEPS_PER_BANK, outer_taps(1, 0, STEPS_PER_BANK, True), middle)
         middles = [multiply_middle(ot, 1) for ot in range(O_TILES)]
-        for ot in range(O_TILES):
-            for d0 in HALVES:
-                acc = outer_taps_of_bank(ot, 1, d0)
-                finish_on_vector(ot, 1, d0, acc, middles[ot])
+        for d0 in HALVES:
+            finish_on_vector(0, 1, d0, outer_taps(0, 1, d0, True), middles[0])
+        first = outer_taps(1, 1, 0, False)
+        add_middle_in_psum(1, 1, first)
+        finish_on_scalar(1, 1, 0, first)
+        n = STEPS_PER_BANK // 2
+        for d in range(STEPS_PER_BANK, N_STEPS, n):
+            finish_on_vector(1, 1, d, outer_taps(1, 1, d, True, n), middles[1], n)

@@ -20,7 +20,7 @@ PIXELS = H * W
 O_TILES = O // P
 STEPS_PER_BANK = 4
 UNMOVED = N_STEPS
-N_COPIES = N_STEPS + 1
+N_COPIES = N_STEPS + STEPS_PER_BANK
 HALVES = (0, STEPS_PER_BANK)
 
 FLOPS = 2 * B * H * W * C * O * TAPS
@@ -82,8 +82,9 @@ def tile_r8convf_pa_s_kernel(tc, x, weight, out):
             for d in steps:
                 quantise_copy(b, d, *STEPS[d])
 
-        def quantise_unmoved(b):
-            quantise_copy(b, UNMOVED, 0, 0)
+        def quantise_unmoved(b, n):
+            for copy in range(UNMOVED, UNMOVED + n):
+                quantise_copy(b, copy, 0, 0)
 
         def sort_weight(ot, k, copy_on_engine):
             copy_on_engine(
@@ -150,8 +151,7 @@ def tile_r8convf_pa_s_kernel(tc, x, weight, out):
             store(ot, b, d0, result)
 
         def add_middle_in_psum(ot, b, acc):
-            for i in range(STEPS_PER_BANK):
-                multiply(acc[:, i : i + 1], ot, b, 1, UNMOVED, False, i == STEPS_PER_BANK - 1)
+            multiply(acc[:], ot, b, 1, UNMOVED, False, True)
 
         def multiply_middle(ot, b):
             product = new_bank()
@@ -210,7 +210,7 @@ def tile_r8convf_pa_s_kernel(tc, x, weight, out):
         quantise_weight(0, 0)
         quantise_steps(0, (6, 7, 4, 5))
         quantise_weight(0, 1)
-        quantise_unmoved(0)
+        quantise_unmoved(0, STEPS_PER_BANK)
         interleave_x(1, vector_copy)
         shift_x(1, 1, scalar_copy)
 
@@ -227,7 +227,7 @@ def tile_r8convf_pa_s_kernel(tc, x, weight, out):
 
         for k in (2, 0, 1):
             quantise_weight(1, k)
-        quantise_unmoved(1)
+        quantise_unmoved(1, 1)
         quantise_steps(1, (2, 6, 0, 1, 7, 3, 4, 5))
 
         first = outer_taps(1, 0, 0, False)
@@ -236,11 +236,8 @@ def tile_r8convf_pa_s_kernel(tc, x, weight, out):
         finish_on_scalar(1, 0, 0, first)
         finish_on_vector(1, 0, STEPS_PER_BANK, outer_taps(1, 0, STEPS_PER_BANK, True), middle)
         middles = [multiply_middle(ot, 1) for ot in range(O_TILES)]
-        for d0 in HALVES:
-            finish_on_vector(0, 1, d0, outer_taps(0, 1, d0, True), middles[0])
-        first = outer_taps(1, 1, 0, False)
-        add_middle_in_psum(1, 1, first)
-        finish_on_scalar(1, 1, 0, first)
-        n = STEPS_PER_BANK // 2
-        for d in range(STEPS_PER_BANK, N_STEPS, n):
-            finish_on_vector(1, 1, d, outer_taps(1, 1, d, True, n), middles[1], n)
+        for ot in range(O_TILES):
+            for d0 in HALVES:
+                n = STEPS_PER_BANK // 2 if (ot, d0) == (O_TILES - 1, HALVES[-1]) else STEPS_PER_BANK
+                for d in range(d0, d0 + STEPS_PER_BANK, n):
+                    finish_on_vector(ot, 1, d, outer_taps(ot, 1, d, True, n), middles[ot], n)

@@ -37,7 +37,6 @@ def tile_r8convf_pa_s_kernel(tc, x, weight, out):
 
         zeros = keep.tile([P, P], F32)
         identity = keep.tile([P, P], F32)
-        identity_bf16 = keep.tile([P, P], BF16)
         x_raw = keep.tile([P, B, PACK, H, W], BF16)
         w_raw = keep.tile([P, O_TILES, C, TAPS], BF16)
         x_moved = keep.tile([P, B, 3, H + 2, W, PACK], BF16, align_bytes=64)
@@ -92,23 +91,14 @@ def tile_r8convf_pa_s_kernel(tc, x, weight, out):
                 in_=w_raw[:, ot, :, k].rearrange("o (p u e) -> o u p e", u=PACK // 2, e=2),
             )
 
-        def transpose_unsorted_weight(ot, k):
-            w_t = psum.tile([P, PACK, P], BF16, tag="bank", name="w_t")
-            for t in range(PACK):
-                nc.tensor.transpose(w_t[:, t, :], w_raw[:, ot, t : C : PACK, k], identity_bf16[:])
-            return w_t
-
-        def group_unsorted_weight(ot, k, w_t):
-            nc.scalar.copy(out=w_grouped[:, ot, k], in_=w_t[:].rearrange("p t o -> p o t"))
-
-        def transpose_sorted_weight(ot, k):
+        def transpose_weight(ot, k):
             w_t = psum.tile([P, PACK // 2, P], F32, tag="bank", name="w_t")
             for u in range(PACK // 2):
                 words = w_pairs[:, ot, k, u].rearrange("o p e -> o (p e)").bitcast(F32)
                 nc.tensor.transpose(w_t[:, u, :], words, identity[:])
             return w_t
 
-        def group_sorted_weight(ot, k, w_t):
+        def group_weight(ot, k, w_t):
             grouped_words = w_grouped[:, ot, k].rearrange("p o t -> p (o t)").bitcast(F32)
             nc.scalar.copy(
                 out=grouped_words.rearrange("p (o u) -> p o u", u=PACK // 2),
@@ -160,20 +150,22 @@ def tile_r8convf_pa_s_kernel(tc, x, weight, out):
             nc.scalar.copy(out=middle[:], in_=product[:, :1])
             return middle
 
-        def finish_on_vector(ot, b, d0, acc, middle, n=STEPS_PER_BANK):
-            result = stage.tile([P, n, PIXELS], F32, tag="result", name="result")
-            nc.vector.tensor_tensor(
-                out=result[:],
-                in0=acc[:, :n],
-                in1=middle[:].to_broadcast([P, n, PIXELS]),
-                op=mybir.AluOpType.add,
-            )
-            store(ot, b, d0, result)
+        def finish_on_vector(ot, b, d0, acc, middle, pieces=1):
+            n = STEPS_PER_BANK // pieces
+            for i in range(0, STEPS_PER_BANK, n):
+                result = stage.tile([P, n, PIXELS], F32, tag="result", name="result")
+                nc.vector.tensor_tensor(
+                    out=result[:],
+                    in0=acc[:, i : i + n],
+                    in1=middle[:].to_broadcast([P, n, PIXELS]),
+                    op=mybir.AluOpType.add,
+                )
+                store(ot, b, d0 + i, result)
 
-        def outer_taps(ot, b, d0, stop, n=STEPS_PER_BANK):
+        def outer_taps(ot, b, d0, stop):
             acc = new_bank()
-            multiply(acc[:, :n], ot, b, 2, d0, True, False)
-            multiply(acc[:, :n], ot, b, 0, (d0 + N_STEPS // 2) % N_STEPS, False, stop)
+            multiply(acc[:], ot, b, 2, d0, True, False)
+            multiply(acc[:], ot, b, 0, (d0 + N_STEPS // 2) % N_STEPS, False, stop)
             return acc
 
         load_x(0)
@@ -184,7 +176,6 @@ def tile_r8convf_pa_s_kernel(tc, x, weight, out):
         unused = psum.tile([P, STEPS_PER_BANK, P], F32, tag="bank", name="unused")
         for i in range(STEPS_PER_BANK):
             nc.tensor.matmul(unused[:, i], zeros[:], zeros[:], start=True, stop=True)
-        make_identity(nc, identity_bf16[:])
         make_identity(nc, identity[:])
         borders = x_moved[:].rearrange("p b a h w t -> p (b a) h (w t)").bitcast(I32)
         nc.vector.memset(borders[:, :, 0 : H + 2 : H + 1], 0)
@@ -193,26 +184,31 @@ def tile_r8convf_pa_s_kernel(tc, x, weight, out):
 
         vector_copy, scalar_copy = nc.vector.tensor_copy, nc.scalar.copy
         interleave_x(0, vector_copy)
-        shift_x(0, -1, scalar_copy)
         shift_x(0, 1, vector_copy)
-        unsorted = transpose_unsorted_weight(0, 1)
-        for k in (2, 0):
-            sort_weight(0, k, vector_copy)
-        for k in (2, 0):
-            group_sorted_weight(0, k, transpose_sorted_weight(0, k))
-        group_unsorted_weight(0, 1, unsorted)
-        quantise_steps(0, (2, 0, 1, 3))
-        for k in (0, 1):
-            group_unsorted_weight(1, k, transpose_unsorted_weight(1, k))
+        shift_x(0, -1, vector_copy)
+        sort_weight(0, 1, scalar_copy)
+        sort_weight(1, 1, scalar_copy)
+        sort_weight(0, 2, vector_copy)
+        sort_weight(0, 0, vector_copy)
+        quantise_steps(0, (2, 0))
         sort_weight(1, 2, vector_copy)
-        group_sorted_weight(1, 2, transpose_sorted_weight(1, 2))
+        sort_weight(1, 0, vector_copy)
+        for ot in range(O_TILES):
+            for k in (2, 0, 1):
+                group_weight(ot, k, transpose_weight(ot, k))
+        quantise_steps(0, (1, 3))
         quantise_weight(0, 2)
         quantise_weight(0, 0)
         quantise_steps(0, (6, 7, 4, 5))
         quantise_weight(0, 1)
         quantise_unmoved(0, STEPS_PER_BANK)
-        interleave_x(1, vector_copy)
+        interleave_x(1, scalar_copy)
         shift_x(1, 1, scalar_copy)
+        for k in (2, 0, 1):
+            quantise_weight(1, k)
+        shift_x(1, -1, vector_copy)
+        quantise_unmoved(1, 1)
+        quantise_steps(1, (2, 6, 3, 4, 5, 0, 1, 7))
 
         first, second = new_bank(), new_bank()
         multiply(first[:], 0, 0, 2, 0, True, False)
@@ -222,14 +218,6 @@ def tile_r8convf_pa_s_kernel(tc, x, weight, out):
         for d0, acc in zip(HALVES, (first, second)):
             add_middle_in_psum(0, 0, acc)
             finish_on_scalar(0, 0, d0, acc)
-            if d0 == 0:
-                shift_x(1, -1, scalar_copy)
-
-        for k in (2, 0, 1):
-            quantise_weight(1, k)
-        quantise_unmoved(1, 1)
-        quantise_steps(1, (2, 6, 0, 1, 7, 3, 4, 5))
-
         first = outer_taps(1, 0, 0, False)
         middle = multiply_middle(1, 0)
         add_middle_in_psum(1, 0, first)
@@ -238,6 +226,5 @@ def tile_r8convf_pa_s_kernel(tc, x, weight, out):
         middles = [multiply_middle(ot, 1) for ot in range(O_TILES)]
         for ot in range(O_TILES):
             for d0 in HALVES:
-                n = STEPS_PER_BANK // 2 if (ot, d0) == (O_TILES - 1, HALVES[-1]) else STEPS_PER_BANK
-                for d in range(d0, d0 + STEPS_PER_BANK, n):
-                    finish_on_vector(ot, 1, d, outer_taps(ot, 1, d, True, n), middles[ot], n)
+                last = (ot, d0) == (O_TILES - 1, HALVES[-1])
+                finish_on_vector(ot, 1, d0, outer_taps(ot, 1, d0, True), middles[ot], 2 if last else 1)

@@ -168,14 +168,14 @@ def tile_r8convf_pa_s_kernel(tc, x, weight, out):
             multiply(acc[:], ot, b, 0, (d0 + N_STEPS // 2) % N_STEPS, False, stop)
             return acc
 
+        def keep_tensor_busy(i):
+            nc.tensor.matmul(unused[:, i], zeros[:], zeros[:], start=True, stop=True)
+
         load_x(0)
         load_weight(0)
         load_weight(1)
         load_x(1)
-        nc.vector.memset(zeros[:], 0.0)
         unused = psum.tile([P, STEPS_PER_BANK, P], F32, tag="bank", name="unused")
-        for i in range(STEPS_PER_BANK):
-            nc.tensor.matmul(unused[:, i], zeros[:], zeros[:], start=True, stop=True)
         make_identity(nc, identity[:])
         borders = x_moved[:].rearrange("p b a h w t -> p (b a) h (w t)").bitcast(I32)
         nc.vector.memset(borders[:, :, 0 : H + 2 : H + 1], 0)
@@ -184,6 +184,7 @@ def tile_r8convf_pa_s_kernel(tc, x, weight, out):
 
         vector_copy, scalar_copy = nc.vector.tensor_copy, nc.scalar.copy
         interleave_x(0, vector_copy)
+        nc.vector.memset(zeros[:], 0.0)
         shift_x(0, 1, vector_copy)
         shift_x(0, -1, vector_copy)
         sort_weight(0, 1, scalar_copy)
@@ -193,9 +194,15 @@ def tile_r8convf_pa_s_kernel(tc, x, weight, out):
         quantise_steps(0, (2, 0))
         sort_weight(1, 2, vector_copy)
         sort_weight(1, 0, vector_copy)
-        for ot in range(O_TILES):
-            for k in (2, 0, 1):
-                group_weight(ot, k, transpose_weight(ot, k))
+        keep_tensor_busy(0)
+        group_weight(0, 2, transpose_weight(0, 2))
+        keep_tensor_busy(1)
+        group_weight(0, 0, transpose_weight(0, 0))
+        group_weight(0, 1, transpose_weight(0, 1))
+        keep_tensor_busy(2)
+        for k in (2, 0, 1):
+            group_weight(1, k, transpose_weight(1, k))
+        keep_tensor_busy(3)
         quantise_steps(0, (1, 3))
         quantise_weight(0, 2)
         quantise_weight(0, 0)

@@ -23,6 +23,8 @@ UNMOVED = N_STEPS
 N_COPIES = N_STEPS + STEPS_PER_BANK
 HALVES = (0, STEPS_PER_BANK)
 
+IDLE_COLUMNS = 300
+
 FLOPS = 2 * B * H * W * C * O * TAPS
 
 
@@ -35,10 +37,10 @@ def tile_r8convf_pa_s_kernel(tc, x, weight, out):
         mid_pool = ctx.enter_context(tc.tile_pool(name="mid_pool", bufs=4))
         psum = ctx.enter_context(tc.psum_pool(name="psum", bufs=8))
 
-        zeros = keep.tile([P, P], F32)
+        zeros = keep.tile([P, IDLE_COLUMNS], F32)
         identity = keep.tile([P, P], F32)
         x_raw = keep.tile([P, B, PACK, H, W], BF16)
-        w_raw = keep.tile([P, O_TILES, C, TAPS], BF16)
+        w_raw = keep.tile([P, O_TILES, C * TAPS], BF16)
         x_moved = keep.tile([P, B, 3, H + 2, W, PACK], BF16, align_bytes=64)
         x_codes = keep.tile([P, B, N_COPIES * PIXELS], U32, align_bytes=64)
         x_scales = keep.tile([P, B, N_COPIES * PIXELS], U8, align_bytes=64)
@@ -55,7 +57,7 @@ def tile_r8convf_pa_s_kernel(tc, x, weight, out):
 
         def load_weight(ot):
             nc.sync.dma_start(
-                out=w_raw[:, ot].rearrange("p c k -> p (c k)"),
+                out=w_raw[:, ot],
                 in_=weight[ot * P : (ot + 1) * P].rearrange("o c k -> o (c k)"),
             )
 
@@ -81,14 +83,22 @@ def tile_r8convf_pa_s_kernel(tc, x, weight, out):
             for d in steps:
                 quantise_copy(b, d, *STEPS[d])
 
-        def quantise_unmoved(b, n):
-            for copy in range(UNMOVED, UNMOVED + n):
-                quantise_copy(b, copy, 0, 0)
+        def quantise_unmoved(b):
+            quantise_copy(b, UNMOVED, 0, 0)
+
+        def repeat_unmoved(b):
+            for tile in (x_codes[:, b].bitcast(I32), x_scales[:, b].bitcast(I32)):
+                n = tile.shape[1] // N_COPIES
+                copies = tile.rearrange("p (d n) -> p d n", n=n)
+                nc.sync.dma_start(
+                    out=copies[:, UNMOVED + 1 :],
+                    in_=copies[:, UNMOVED : UNMOVED + 1].to_broadcast([P, STEPS_PER_BANK - 1, n]),
+                )
 
         def sort_weight(ot, k, copy_on_engine):
             copy_on_engine(
                 out=w_pairs[:, ot, k],
-                in_=w_raw[:, ot, :, k].rearrange("o (p u e) -> o u p e", u=PACK // 2, e=2),
+                in_=w_raw[:, ot].rearrange("o (p u e k) -> o k u p e", u=PACK // 2, e=2, k=TAPS)[:, k],
             )
 
         def transpose_weight(ot, k):
@@ -168,24 +178,27 @@ def tile_r8convf_pa_s_kernel(tc, x, weight, out):
             multiply(acc[:], ot, b, 0, (d0 + N_STEPS // 2) % N_STEPS, False, stop)
             return acc
 
-        def keep_tensor_busy(i):
-            nc.tensor.matmul(unused[:, i], zeros[:], zeros[:], start=True, stop=True)
+        def keep_tensor_busy(stationary):
+            nc.tensor.matmul(unused[:], stationary, zeros[:], start=True, stop=True)
 
         load_x(0)
         load_weight(0)
         load_weight(1)
         load_x(1)
-        unused = psum.tile([P, STEPS_PER_BANK, P], F32, tag="bank", name="unused")
+        unused = psum.tile([P, IDLE_COLUMNS], F32, tag="bank", name="unused")
         make_identity(nc, identity[:])
+        nc.gpsimd.memset(x_scales[:, 0, UNMOVED * PIXELS : (UNMOVED + 1) * PIXELS].bitcast(I32), 0)
         borders = x_moved[:].rearrange("p b a h w t -> p (b a) h (w t)").bitcast(I32)
         nc.vector.memset(borders[:, :, 0 : H + 2 : H + 1], 0)
         nc.vector.memset(borders[:, 0 : 3 * B : 3, 1 : 1 + H, :2], 0)
         nc.vector.memset(borders[:, 2 : 3 * B : 3, 1 : 1 + H, 2 * W - 2 :], 0)
+        nc.vector.memset(zeros[:], 0.0)
 
         vector_copy, scalar_copy = nc.vector.tensor_copy, nc.scalar.copy
         interleave_x(0, vector_copy)
-        nc.vector.memset(zeros[:], 0.0)
         shift_x(0, 1, vector_copy)
+        quantise_unmoved(0)
+        repeat_unmoved(0)
         shift_x(0, -1, vector_copy)
         sort_weight(0, 1, scalar_copy)
         sort_weight(1, 1, scalar_copy)
@@ -194,27 +207,22 @@ def tile_r8convf_pa_s_kernel(tc, x, weight, out):
         quantise_steps(0, (2, 0))
         sort_weight(1, 2, vector_copy)
         sort_weight(1, 0, vector_copy)
-        keep_tensor_busy(0)
-        group_weight(0, 2, transpose_weight(0, 2))
-        keep_tensor_busy(1)
-        group_weight(0, 0, transpose_weight(0, 0))
-        group_weight(0, 1, transpose_weight(0, 1))
-        keep_tensor_busy(2)
-        for k in (2, 0, 1):
-            group_weight(1, k, transpose_weight(1, k))
-        keep_tensor_busy(3)
+        keep_tensor_busy(zeros[:, :P])
+        keep_tensor_busy(w_raw[:, 0].bitcast(F32)[:, :P])
+        for ot in range(O_TILES):
+            for k in (2, 0, 1):
+                group_weight(ot, k, transpose_weight(ot, k))
         quantise_steps(0, (1, 3))
         quantise_weight(0, 2)
         quantise_weight(0, 0)
         quantise_steps(0, (6, 7, 4, 5))
         quantise_weight(0, 1)
-        quantise_unmoved(0, STEPS_PER_BANK)
         interleave_x(1, scalar_copy)
         shift_x(1, 1, scalar_copy)
         for k in (2, 0, 1):
             quantise_weight(1, k)
         shift_x(1, -1, vector_copy)
-        quantise_unmoved(1, 1)
+        quantise_unmoved(1)
         quantise_steps(1, (2, 6, 3, 4, 5, 0, 1, 7))
 
         first, second = new_bank(), new_bank()

@@ -23,7 +23,7 @@ UNMOVED = N_STEPS
 N_COPIES = N_STEPS + STEPS_PER_BANK
 HALVES = (0, STEPS_PER_BANK)
 
-IDLE_COLUMNS = 300
+IDLE_COLUMNS = 152
 
 FLOPS = 2 * B * H * W * C * O * TAPS
 
@@ -44,6 +44,8 @@ def tile_r8convf_pa_s_kernel(tc, x, weight, out):
         x_moved = keep.tile([P, B, 3, H + 2, W, PACK], BF16, align_bytes=64)
         x_codes = keep.tile([P, B, N_COPIES * PIXELS], U32, align_bytes=64)
         x_scales = keep.tile([P, B, N_COPIES * PIXELS], U8, align_bytes=64)
+        unmoved_codes = keep.tile([P, B * PIXELS], U32, align_bytes=64)
+        unmoved_scales = keep.tile([P, B * PIXELS], U8, align_bytes=64)
         w_pairs = keep.tile([P, O_TILES, TAPS, PACK // 2, P, 2], BF16, align_bytes=64)
         w_grouped = keep.tile([P, O_TILES, TAPS, P, PACK], BF16, align_bytes=64)
         w_codes = keep.tile([P, O_TILES, TAPS, P], U32, align_bytes=64)
@@ -71,28 +73,29 @@ def tile_r8convf_pa_s_kernel(tc, x, weight, out):
                 in_=x_moved[:, b, 1, 1 : 1 + H, first + dx : last + dx],
             )
 
-        def quantise_copy(b, copy, dy, dx):
-            columns = slice(copy * PIXELS, (copy + 1) * PIXELS)
+        def quantise_moved(b, dy, dx, codes, scales):
             nc.vector.quantize_mx(
-                out=x_codes[:, b, columns].bitcast(FP8X4),
-                scales=x_scales[:, b, columns],
+                out=codes.bitcast(FP8X4),
+                scales=scales,
                 in_=x_moved[:, b, dx + 1, 1 + dy : 1 + dy + H].rearrange("p h w t -> p (h w t)"),
             )
 
         def quantise_steps(b, steps):
             for d in steps:
-                quantise_copy(b, d, *STEPS[d])
+                columns = slice(d * PIXELS, (d + 1) * PIXELS)
+                quantise_moved(b, *STEPS[d], x_codes[:, b, columns], x_scales[:, b, columns])
 
         def quantise_unmoved(b):
-            quantise_copy(b, UNMOVED, 0, 0)
+            columns = slice(b * PIXELS, (b + 1) * PIXELS)
+            quantise_moved(b, 0, 0, unmoved_codes[:, columns], unmoved_scales[:, columns])
 
         def repeat_unmoved(b):
-            for tile in (x_codes[:, b].bitcast(I32), x_scales[:, b].bitcast(I32)):
-                n = tile.shape[1] // N_COPIES
-                copies = tile.rearrange("p (d n) -> p d n", n=n)
+            for copies, unmoved in ((x_codes[:, b], unmoved_codes), (x_scales[:, b], unmoved_scales)):
+                copies, unmoved = copies.bitcast(I32), unmoved[:].bitcast(I32)
+                n = unmoved.shape[1] // B
                 nc.sync.dma_start(
-                    out=copies[:, UNMOVED + 1 :],
-                    in_=copies[:, UNMOVED : UNMOVED + 1].to_broadcast([P, STEPS_PER_BANK - 1, n]),
+                    out=copies[:, UNMOVED * n :].rearrange("p (i n) -> p i n", n=n),
+                    in_=unmoved[:, b * n : (b + 1) * n].unsqueeze(1).to_broadcast([P, STEPS_PER_BANK, n]),
                 )
 
         def sort_weight(ot, k, copy_on_engine):
@@ -126,17 +129,21 @@ def tile_r8convf_pa_s_kernel(tc, x, weight, out):
             acc = psum.tile([P, STEPS_PER_BANK, PIXELS], F32, tag="bank", name="acc")
             return acc
 
-        def multiply(product, ot, b, k, first_copy, start, stop):
-            columns = slice(first_copy * PIXELS, (first_copy + product.shape[1]) * PIXELS)
+        def multiply_columns(product, ot, k, codes, scales, start, stop):
             nc.tensor.matmul_mx(
-                out=product.rearrange("p d n -> p (d n)"),
+                out=product,
                 lhsT=w_codes[:, ot, k].bitcast(FP8X4),
                 lhsT_scale=w_scales[:, ot, k],
-                rhs=x_codes[:, b, columns].bitcast(FP8X4),
-                rhs_scale=x_scales[:, b, columns],
+                rhs=codes.bitcast(FP8X4),
+                rhs_scale=scales,
                 start=start,
                 stop=stop,
             )
+
+        def multiply(acc, ot, b, k, first_copy, start, stop):
+            columns = slice(first_copy * PIXELS, (first_copy + STEPS_PER_BANK) * PIXELS)
+            bank = acc[:].rearrange("p d n -> p (d n)")
+            multiply_columns(bank, ot, k, x_codes[:, b, columns], x_scales[:, b, columns], start, stop)
 
         def store(ot, b, d0, result):
             n = result.shape[1]
@@ -151,14 +158,17 @@ def tile_r8convf_pa_s_kernel(tc, x, weight, out):
             store(ot, b, d0, result)
 
         def add_middle_in_psum(ot, b, acc):
-            multiply(acc[:], ot, b, 1, UNMOVED, False, True)
+            multiply(acc, ot, b, 1, UNMOVED, False, True)
 
-        def multiply_middle(ot, b):
+        def multiply_middle(ot, first_image):
+            columns = slice(first_image * PIXELS, B * PIXELS)
             product = new_bank()
-            multiply(product[:, :1], ot, b, 1, UNMOVED, True, True)
-            middle = mid_pool.tile([P, 1, PIXELS], F32, tag="middle", name="middle")
-            nc.scalar.copy(out=middle[:], in_=product[:, :1])
-            return middle
+            n = B - first_image
+            bank = product[:, :n].rearrange("p i n -> p (i n)")
+            multiply_columns(bank, ot, 1, unmoved_codes[:, columns], unmoved_scales[:, columns], True, True)
+            middle = mid_pool.tile([P, n, PIXELS], F32, tag="middle", name="middle")
+            nc.scalar.copy(out=middle[:], in_=product[:, :n])
+            return [middle[:, i : i + 1] for i in range(n)]
 
         def finish_on_vector(ot, b, d0, acc, middle, pieces=1):
             n = STEPS_PER_BANK // pieces
@@ -167,15 +177,15 @@ def tile_r8convf_pa_s_kernel(tc, x, weight, out):
                 nc.vector.tensor_tensor(
                     out=result[:],
                     in0=acc[:, i : i + n],
-                    in1=middle[:].to_broadcast([P, n, PIXELS]),
+                    in1=middle.to_broadcast([P, n, PIXELS]),
                     op=mybir.AluOpType.add,
                 )
                 store(ot, b, d0 + i, result)
 
         def outer_taps(ot, b, d0, stop):
             acc = new_bank()
-            multiply(acc[:], ot, b, 2, d0, True, False)
-            multiply(acc[:], ot, b, 0, (d0 + N_STEPS // 2) % N_STEPS, False, stop)
+            multiply(acc, ot, b, 2, d0, True, False)
+            multiply(acc, ot, b, 0, (d0 + N_STEPS // 2) % N_STEPS, False, stop)
             return acc
 
         def keep_tensor_busy(stationary):
@@ -187,31 +197,35 @@ def tile_r8convf_pa_s_kernel(tc, x, weight, out):
         load_x(1)
         unused = psum.tile([P, IDLE_COLUMNS], F32, tag="bank", name="unused")
         make_identity(nc, identity[:])
-        nc.gpsimd.memset(x_scales[:, 0, UNMOVED * PIXELS : (UNMOVED + 1) * PIXELS].bitcast(I32), 0)
+        nc.gpsimd.memset(unmoved_scales[:].bitcast(I32), 0)
+        nc.gpsimd.memset(zeros[:], 0.0)
         borders = x_moved[:].rearrange("p b a h w t -> p (b a) h (w t)").bitcast(I32)
         nc.vector.memset(borders[:, :, 0 : H + 2 : H + 1], 0)
         nc.vector.memset(borders[:, 0 : 3 * B : 3, 1 : 1 + H, :2], 0)
         nc.vector.memset(borders[:, 2 : 3 * B : 3, 1 : 1 + H, 2 * W - 2 :], 0)
-        nc.vector.memset(zeros[:], 0.0)
 
         vector_copy, scalar_copy = nc.vector.tensor_copy, nc.scalar.copy
         interleave_x(0, vector_copy)
         shift_x(0, 1, vector_copy)
-        quantise_unmoved(0)
-        repeat_unmoved(0)
         shift_x(0, -1, vector_copy)
         sort_weight(0, 1, scalar_copy)
         sort_weight(1, 1, scalar_copy)
         sort_weight(0, 2, vector_copy)
         sort_weight(0, 0, vector_copy)
+        quantise_unmoved(0)
+        repeat_unmoved(0)
         quantise_steps(0, (2, 0))
         sort_weight(1, 2, vector_copy)
         sort_weight(1, 0, vector_copy)
         keep_tensor_busy(zeros[:, :P])
-        keep_tensor_busy(w_raw[:, 0].bitcast(F32)[:, :P])
-        for ot in range(O_TILES):
-            for k in (2, 0, 1):
-                group_weight(ot, k, transpose_weight(ot, k))
+        keep_tensor_busy(x_raw[:, 0].rearrange("p t h w -> p (t h w)").bitcast(F32)[:, :P])
+        group_weight(0, 2, transpose_weight(0, 2))
+        keep_tensor_busy(w_pairs[:, 0, 2, 0].rearrange("o p e -> o (p e)").bitcast(F32))
+        for k in (0, 1):
+            group_weight(0, k, transpose_weight(0, k))
+        keep_tensor_busy(zeros[:, :P])
+        for k in (2, 0, 1):
+            group_weight(1, k, transpose_weight(1, k))
         quantise_steps(0, (1, 3))
         quantise_weight(0, 2)
         quantise_weight(0, 0)
@@ -226,20 +240,20 @@ def tile_r8convf_pa_s_kernel(tc, x, weight, out):
         quantise_steps(1, (2, 6, 3, 4, 5, 0, 1, 7))
 
         first, second = new_bank(), new_bank()
-        multiply(first[:], 0, 0, 2, 0, True, False)
-        multiply(second[:], 0, 0, 0, 0, True, False)
-        multiply(first[:], 0, 0, 0, STEPS_PER_BANK, False, False)
-        multiply(second[:], 0, 0, 2, STEPS_PER_BANK, False, False)
+        multiply(first, 0, 0, 2, 0, True, False)
+        multiply(second, 0, 0, 0, 0, True, False)
+        multiply(first, 0, 0, 0, STEPS_PER_BANK, False, False)
+        multiply(second, 0, 0, 2, STEPS_PER_BANK, False, False)
         for d0, acc in zip(HALVES, (first, second)):
             add_middle_in_psum(0, 0, acc)
             finish_on_scalar(0, 0, d0, acc)
+        acc = outer_taps(1, 0, STEPS_PER_BANK, True)
+        middles = {ot: multiply_middle(ot, first_image) for ot, first_image in ((1, 0), (0, 1))}
+        finish_on_vector(1, 0, STEPS_PER_BANK, acc, middles[1][0])
         first = outer_taps(1, 0, 0, False)
-        middle = multiply_middle(1, 0)
         add_middle_in_psum(1, 0, first)
         finish_on_scalar(1, 0, 0, first)
-        finish_on_vector(1, 0, STEPS_PER_BANK, outer_taps(1, 0, STEPS_PER_BANK, True), middle)
-        middles = [multiply_middle(ot, 1) for ot in range(O_TILES)]
         for ot in range(O_TILES):
             for d0 in HALVES:
                 last = (ot, d0) == (O_TILES - 1, HALVES[-1])
-                finish_on_vector(ot, 1, d0, outer_taps(ot, 1, d0, True), middles[ot], 2 if last else 1)
+                finish_on_vector(ot, 1, d0, outer_taps(ot, 1, d0, True), middles[ot][-1], 2 if last else 1)

@@ -207,13 +207,13 @@ def tile_r8convf_pa_s_kernel(tc, x, weight, out):
         vector_copy, scalar_copy = nc.vector.tensor_copy, nc.scalar.copy
         interleave_x(0, vector_copy)
         shift_x(0, 1, vector_copy)
+        quantise_unmoved(0)
+        repeat_unmoved(0)
         shift_x(0, -1, vector_copy)
         sort_weight(0, 1, scalar_copy)
         sort_weight(1, 1, scalar_copy)
         sort_weight(0, 2, vector_copy)
         sort_weight(0, 0, vector_copy)
-        quantise_unmoved(0)
-        repeat_unmoved(0)
         quantise_steps(0, (2, 0))
         sort_weight(1, 2, vector_copy)
         sort_weight(1, 0, vector_copy)
@@ -232,10 +232,10 @@ def tile_r8convf_pa_s_kernel(tc, x, weight, out):
         quantise_steps(0, (6, 7, 4, 5))
         quantise_weight(0, 1)
         interleave_x(1, scalar_copy)
-        shift_x(1, 1, scalar_copy)
         for k in (2, 0, 1):
             quantise_weight(1, k)
         shift_x(1, -1, vector_copy)
+        shift_x(1, 1, vector_copy)
         quantise_unmoved(1)
         quantise_steps(1, (2, 6, 3, 4, 5, 0, 1, 7))
 
@@ -243,16 +243,16 @@ def tile_r8convf_pa_s_kernel(tc, x, weight, out):
         multiply(first, 0, 0, 2, 0, True, False)
         multiply(second, 0, 0, 0, 0, True, False)
         multiply(first, 0, 0, 0, STEPS_PER_BANK, False, False)
+        add_middle_in_psum(0, 0, first)
+        finish_on_scalar(0, 0, 0, first)
         multiply(second, 0, 0, 2, STEPS_PER_BANK, False, False)
-        for d0, acc in zip(HALVES, (first, second)):
-            add_middle_in_psum(0, 0, acc)
-            finish_on_scalar(0, 0, d0, acc)
-        acc = outer_taps(1, 0, STEPS_PER_BANK, True)
-        middles = {ot: multiply_middle(ot, first_image) for ot, first_image in ((1, 0), (0, 1))}
-        finish_on_vector(1, 0, STEPS_PER_BANK, acc, middles[1][0])
+        add_middle_in_psum(0, 0, second)
+        finish_on_scalar(0, 0, STEPS_PER_BANK, second)
         first = outer_taps(1, 0, 0, False)
+        middles = {ot: multiply_middle(ot, first_image) for ot, first_image in ((1, 0), (0, 1))}
         add_middle_in_psum(1, 0, first)
         finish_on_scalar(1, 0, 0, first)
+        finish_on_vector(1, 0, STEPS_PER_BANK, outer_taps(1, 0, STEPS_PER_BANK, True), middles[1][0])
         for ot in range(O_TILES):
             for d0 in HALVES:
                 last = (ot, d0) == (O_TILES - 1, HALVES[-1])

from contextlib import ExitStack

import concourse.mybir as mybir
from concourse.masks import make_identity

BF16 = mybir.dt.bfloat16
F32 = mybir.dt.float32
I32 = mybir.dt.int32
U32 = mybir.dt.uint32
U8 = mybir.dt.uint8
FP8X4 = mybir.dt.float8_e4m3fn_x4

B, C, H, W, O, TAPS = 2, 512, 8, 16, 256, 3
STEPS = ((0, 1), (1, 1), (1, 0), (1, -1), (0, -1), (-1, -1), (-1, 0), (-1, 1))
N_STEPS = len(STEPS)

P = 128
PACK = 4
PIXELS = H * W
O_TILES = O // P
STEPS_PER_BANK = 4
UNMOVED = N_STEPS
N_COPIES = N_STEPS + STEPS_PER_BANK
HALVES = (0, STEPS_PER_BANK)

IDLE_COLUMNS = 152

FLOPS = 2 * B * H * W * C * O * TAPS


def tile_r8convf_pa_s_kernel(tc, x, weight, out):
    nc = tc.nc
    with ExitStack() as ctx:
        ctx.enter_context(tc.manual_schedule())
        keep = ctx.enter_context(tc.tile_pool(name="keep", bufs=1))
        stage = ctx.enter_context(tc.tile_pool(name="stage", bufs=8))
        mid_pool = ctx.enter_context(tc.tile_pool(name="mid_pool", bufs=4))
        psum = ctx.enter_context(tc.psum_pool(name="psum", bufs=8))

        zeros = keep.tile([P, IDLE_COLUMNS], F32)
        identity = keep.tile([P, P], F32)
        x_raw = keep.tile([P, B, PACK, H, W], BF16)
        w_raw = keep.tile([P, O_TILES, C * TAPS], BF16)
        x_moved = keep.tile([P, B, 3, H + 2, W, PACK], BF16, align_bytes=64)
        x_codes = keep.tile([P, B, N_COPIES * PIXELS], U32, align_bytes=64)
        x_scales = keep.tile([P, B, N_COPIES * PIXELS], U8, align_bytes=64)
        unmoved_codes = keep.tile([P, B * PIXELS], U32, align_bytes=64)
        unmoved_scales = keep.tile([P, B * PIXELS], U8, align_bytes=64)
        w_pairs = keep.tile([P, O_TILES, TAPS, PACK // 2, P, 2], BF16, align_bytes=64)
        w_grouped = keep.tile([P, O_TILES, TAPS, P, PACK], BF16, align_bytes=64)
        w_codes = keep.tile([P, O_TILES, TAPS, P], U32, align_bytes=64)
        w_scales = keep.tile([P, O_TILES, TAPS, P], U8, align_bytes=64)

        def load_x(b):
            nc.sync.dma_start(
                out=x_raw[:, b].rearrange("p t h w -> p t (h w)"),
                in_=x[b].rearrange("(p t) h w -> p t (h w)", t=PACK),
            )

        def load_weight(ot):
            nc.sync.dma_start(
                out=w_raw[:, ot],
                in_=weight[ot * P : (ot + 1) * P].rearrange("o c k -> o (c k)"),
            )

        def interleave_x(b, copy_on_engine):
            copy_on_engine(out=x_moved[:, b, 1, 1 : 1 + H], in_=x_raw[:, b].rearrange("p t h w -> p h w t"))

        def shift_x(b, dx, copy_on_engine):
            first, last = max(0, -dx), W - max(0, dx)
            copy_on_engine(
                out=x_moved[:, b, dx + 1, 1 : 1 + H, first:last],
                in_=x_moved[:, b, 1, 1 : 1 + H, first + dx : last + dx],
            )

        def quantise_moved(b, dy, dx, codes, scales):
            nc.vector.quantize_mx(
                out=codes.bitcast(FP8X4),
                scales=scales,
                in_=x_moved[:, b, dx + 1, 1 + dy : 1 + dy + H].rearrange("p h w t -> p (h w t)"),
            )

        def quantise_steps(b, steps):
            for d in steps:
                columns = slice(d * PIXELS, (d + 1) * PIXELS)
                quantise_moved(b, *STEPS[d], x_codes[:, b, columns], x_scales[:, b, columns])

        def quantise_unmoved(b):
            columns = slice(b * PIXELS, (b + 1) * PIXELS)
            quantise_moved(b, 0, 0, unmoved_codes[:, columns], unmoved_scales[:, columns])

        def repeat_unmoved(b):
            for copies, unmoved in ((x_codes[:, b], unmoved_codes), (x_scales[:, b], unmoved_scales)):
                copies, unmoved = copies.bitcast(I32), unmoved[:].bitcast(I32)
                n = unmoved.shape[1] // B
                nc.sync.dma_start(
                    out=copies[:, UNMOVED * n :].rearrange("p (i n) -> p i n", n=n),
                    in_=unmoved[:, b * n : (b + 1) * n].unsqueeze(1).to_broadcast([P, STEPS_PER_BANK, n]),
                )

        def sort_weight(ot, k, copy_on_engine):
            copy_on_engine(
                out=w_pairs[:, ot, k],
                in_=w_raw[:, ot].rearrange("o (p u e k) -> o k u p e", u=PACK // 2, e=2, k=TAPS)[:, k],
            )

        def transpose_weight(ot, k):
            w_t = psum.tile([P, PACK // 2, P], F32, tag="bank", name="w_t")
            for u in range(PACK // 2):
                words = w_pairs[:, ot, k, u].rearrange("o p e -> o (p e)").bitcast(F32)
                nc.tensor.transpose(w_t[:, u, :], words, identity[:])
            return w_t

        def group_weight(ot, k, w_t):
            grouped_words = w_grouped[:, ot, k].rearrange("p o t -> p (o t)").bitcast(F32)
            nc.scalar.copy(
                out=grouped_words.rearrange("p (o u) -> p o u", u=PACK // 2),
                in_=w_t[:].rearrange("p u o -> p o u"),
            )

        def quantise_weight(ot, k):
            nc.vector.quantize_mx(
                out=w_codes[:, ot, k].bitcast(FP8X4),
                scales=w_scales[:, ot, k],
                in_=w_grouped[:, ot, k].rearrange("p o t -> p (o t)"),
            )

        def new_bank():
            acc = psum.tile([P, STEPS_PER_BANK, PIXELS], F32, tag="bank", name="acc")
            return acc

        def multiply_columns(product, ot, k, codes, scales, start, stop):
            nc.tensor.matmul_mx(
                out=product,
                lhsT=w_codes[:, ot, k].bitcast(FP8X4),
                lhsT_scale=w_scales[:, ot, k],
                rhs=codes.bitcast(FP8X4),
                rhs_scale=scales,
                start=start,
                stop=stop,
            )

        def multiply(acc, ot, b, k, first_copy, start, stop):
            columns = slice(first_copy * PIXELS, (first_copy + STEPS_PER_BANK) * PIXELS)
            bank = acc[:].rearrange("p d n -> p (d n)")
            multiply_columns(bank, ot, k, x_codes[:, b, columns], x_scales[:, b, columns], start, stop)

        def store(ot, b, d0, result):
            n = result.shape[1]
            nc.sync.dma_start(
                out=out[b, ot * P : (ot + 1) * P, d0 : d0 + n].rearrange("o d h w -> o d (h w)"),
                in_=result[:],
            )

        def finish_on_scalar(ot, b, d0, acc):
            result = stage.tile([P, STEPS_PER_BANK, PIXELS], F32, tag="result", name="result")
            nc.scalar.copy(out=result[:], in_=acc[:])
            store(ot, b, d0, result)

        def add_middle_in_psum(ot, b, acc):
            multiply(acc, ot, b, 1, UNMOVED, False, True)

        def multiply_middle(ot, first_image):
            columns = slice(first_image * PIXELS, B * PIXELS)
            product = new_bank()
            n = B - first_image
            bank = product[:, :n].rearrange("p i n -> p (i n)")
            multiply_columns(bank, ot, 1, unmoved_codes[:, columns], unmoved_scales[:, columns], True, True)
            middle = mid_pool.tile([P, n, PIXELS], F32, tag="middle", name="middle")
            nc.scalar.copy(out=middle[:], in_=product[:, :n])
            return [middle[:, i : i + 1] for i in range(n)]

        def finish_on_vector(ot, b, d0, acc, middle, pieces=1):
            n = STEPS_PER_BANK // pieces
            for i in range(0, STEPS_PER_BANK, n):
                result = stage.tile([P, n, PIXELS], F32, tag="result", name="result")
                nc.vector.tensor_tensor(
                    out=result[:],
                    in0=acc[:, i : i + n],
                    in1=middle.to_broadcast([P, n, PIXELS]),
                    op=mybir.AluOpType.add,
                )
                store(ot, b, d0 + i, result)

        def outer_taps(ot, b, d0, stop):
            acc = new_bank()
            multiply(acc, ot, b, 2, d0, True, False)
            multiply(acc, ot, b, 0, (d0 + N_STEPS // 2) % N_STEPS, False, stop)
            return acc

        def keep_tensor_busy(stationary):
            nc.tensor.matmul(unused[:], stationary, zeros[:], start=True, stop=True)

        load_x(0)
        load_weight(0)
        load_weight(1)
        load_x(1)
        unused = psum.tile([P, IDLE_COLUMNS], F32, tag="bank", name="unused")
        make_identity(nc, identity[:])
        nc.gpsimd.memset(unmoved_scales[:].bitcast(I32), 0)
        nc.gpsimd.memset(zeros[:], 0.0)
        borders = x_moved[:].rearrange("p b a h w t -> p (b a) h (w t)").bitcast(I32)
        nc.vector.memset(borders[:, :, 0 : H + 2 : H + 1], 0)
        nc.vector.memset(borders[:, 0 : 3 * B : 3, 1 : 1 + H, :2], 0)
        nc.vector.memset(borders[:, 2 : 3 * B : 3, 1 : 1 + H, 2 * W - 2 :], 0)

        vector_copy, scalar_copy = nc.vector.tensor_copy, nc.scalar.copy
        interleave_x(0, vector_copy)
        shift_x(0, 1, vector_copy)
        quantise_unmoved(0)
        repeat_unmoved(0)
        shift_x(0, -1, vector_copy)
        sort_weight(0, 1, scalar_copy)
        sort_weight(1, 1, scalar_copy)
        sort_weight(0, 2, vector_copy)
        sort_weight(0, 0, vector_copy)
        quantise_steps(0, (2, 0))
        sort_weight(1, 2, vector_copy)
        sort_weight(1, 0, vector_copy)
        keep_tensor_busy(zeros[:, :P])
        keep_tensor_busy(x_raw[:, 0].rearrange("p t h w -> p (t h w)").bitcast(F32)[:, :P])
        group_weight(0, 2, transpose_weight(0, 2))
        keep_tensor_busy(w_pairs[:, 0, 2, 0].rearrange("o p e -> o (p e)").bitcast(F32))
        for k in (0, 1):
            group_weight(0, k, transpose_weight(0, k))
        keep_tensor_busy(zeros[:, :P])
        for k in (2, 0, 1):
            group_weight(1, k, transpose_weight(1, k))
        quantise_steps(0, (1, 3))
        quantise_weight(0, 2)
        quantise_weight(0, 0)
        quantise_steps(0, (6, 7, 4, 5))
        quantise_weight(0, 1)
        interleave_x(1, scalar_copy)
        for k in (2, 0, 1):
            quantise_weight(1, k)
        shift_x(1, -1, vector_copy)
        shift_x(1, 1, vector_copy)
        quantise_unmoved(1)
        quantise_steps(1, (2, 6, 3, 4, 5, 0, 1, 7))

        first, second = new_bank(), new_bank()
        multiply(first, 0, 0, 2, 0, True, False)
        multiply(second, 0, 0, 0, 0, True, False)
        multiply(first, 0, 0, 0, STEPS_PER_BANK, False, False)
        add_middle_in_psum(0, 0, first)
        finish_on_scalar(0, 0, 0, first)
        multiply(second, 0, 0, 2, STEPS_PER_BANK, False, False)
        add_middle_in_psum(0, 0, second)
        finish_on_scalar(0, 0, STEPS_PER_BANK, second)
        first = outer_taps(1, 0, 0, False)
        middles = {ot: multiply_middle(ot, first_image) for ot, first_image in ((1, 0), (0, 1))}
        add_middle_in_psum(1, 0, first)
        finish_on_scalar(1, 0, 0, first)
        finish_on_vector(1, 0, STEPS_PER_BANK, outer_taps(1, 0, STEPS_PER_BANK, True), middles[1][0])
        for ot in range(O_TILES):
            for d0 in HALVES:
                last = (ot, d0) == (O_TILES - 1, HALVES[-1])
                finish_on_vector(ot, 1, d0, outer_taps(ot, 1, d0, True), middles[ot][-1], 2 if last else 1)
